import numpy as np
import ml_dtypes


def mxq(x, axis, fmt="e4m3"):
    dtype, down = {"e4m3": (ml_dtypes.float8_e4m3fn, 7), "e5m2": (ml_dtypes.float8_e5m2, 14)}[fmt]
    v = np.moveaxis(np.asarray(x, np.float32).astype(ml_dtypes.bfloat16).astype(np.float64), axis, -1)
    blocks = v.reshape(v.shape[:-1] + (-1, 32))
    amax = np.abs(blocks).max(-1, keepdims=True)
    byte = np.maximum(np.where(amax > 0, np.frexp(amax)[1] - 1 + 127, 0) - down, 1)
    scale = np.exp2(byte - 127.0)
    codes = (blocks / scale).astype(np.float32).astype(dtype).astype(np.float64)
    return np.moveaxis((codes * scale).reshape(v.shape), -1, axis)


WIDE = False


def mx_kscale(k):
    if not WIDE:
        return np.ones(k)
    levels = np.array([10, -10, 5, -5, 0])
    if k % 512:
        return np.exp2(np.random.permutation(np.resize(levels, k // 32))).repeat(32)
    a = np.empty((k // 512, 16))
    for p in range(k // 512):
        a[p, :8] = np.random.permutation(np.resize(levels, 8))
        for g in range(8):
            far = levels[np.abs(levels - a[p, g]) >= 10]
            a[p, g + 8] = far[np.random.randint(len(far))]
    return np.exp2(a.ravel()).repeat(32)


BF16 = ml_dtypes.bfloat16


def bf(x):
    return np.asarray(x, np.float32).astype(BF16)


def f64(x):
    return np.asarray(x).astype(np.float64)


B, S, E, H, D, F = 2, 256, 1024, 8, 128, 4096
EPS = 1e-6
QUIET = 1e-3


def rmsnorm(x, scale):
    ms = np.mean(np.square(x), axis=-1, keepdims=True)
    return x * (1.0 / np.sqrt(ms + EPS)) * scale


def setup_inputs():
    s = mx_kscale(E)
    amp = np.where(np.random.random((B, S, 1)) < 0.25, QUIET, 1.0)
    return {"x": bf(np.random.standard_normal((B, S, E)) * amp),
            "scale1": bf(np.random.standard_normal(E) * s),
            "w_qkv": bf(np.random.standard_normal((E, H, 3 * D)) / np.sqrt(E) / s[:, None, None])}


def reference(x, scale1, w_qkv):
    xn = rmsnorm(f64(x), f64(scale1)).reshape(B * S, E)
    qkv = (mxq(xn, 1, "e4m3") @ mxq(f64(w_qkv).reshape(E, H * 3 * D), 0, "e4m3")).reshape(B, S, H, 3 * D)
    q, k, v = np.split(qkv, 3, axis=-1)
    return q, k, v

@@ -1,0 +1,211 @@
+from contextlib import ExitStack
+
+import concourse.mybir as mybir
+from concourse.masks import make_identity
+
+F32 = mybir.dt.float32
+BF16 = mybir.dt.bfloat16
+U32 = mybir.dt.uint32
+U8 = mybir.dt.uint8
+FP8X4 = mybir.dt.float8_e4m3fn_x4
+ACT = mybir.ActivationFunctionType
+ALU = mybir.AluOpType
+
+P = 128
+PACK = 4
+PAIRS = PACK // 2
+K_PASS = P * PACK
+
+ROWS = 512
+E = 1024
+HEADS = 8
+D = 128
+PARTS = 3
+EPS = 1e-6
+
+ROW_TILES = ROWS // P
+PASSES = E // K_PASS
+N_BLOCK = 512
+HEADS_PER_BLOCK = N_BLOCK // D
+HALVES = HEADS // HEADS_PER_BLOCK
+HALF_COLS = HEADS_PER_BLOCK * PARTS * D
+RUN = 4
+
+FLOPS = 2 * ROWS * E * HEADS * PARTS * D
+
+
+def tile_block_pa_kernel(tc, x, scale1, w_qkv, out_0, out_1, out_2):
+    nc = tc.nc
+    x_rows = x.rearrange("b s e -> (b s) e")
+    w_rows = w_qkv.rearrange("e h c -> e (h c)")
+    out_rows = [o.rearrange("b s h d -> (b s) (h d)") for o in (out_0, out_1, out_2)]
+
+    with ExitStack() as ctx:
+        consts = ctx.enter_context(tc.tile_pool(name="consts", bufs=1))
+        x_pool = ctx.enter_context(tc.tile_pool(name="x_pool", bufs=ROW_TILES))
+        w_pool = ctx.enter_context(tc.tile_pool(name="w_pool", bufs=PASSES * HALVES))
+        mx_pool = ctx.enter_context(tc.tile_pool(name="mx_pool", bufs=1))
+        stage = ctx.enter_context(tc.tile_pool(name="stage", bufs=3))
+        res_pool = ctx.enter_context(tc.tile_pool(name="res_pool", bufs=8))
+        psum = ctx.enter_context(tc.psum_pool(name="psum", bufs=8))
+
+        gain_row = consts.tile([P, E], BF16)
+        nc.vector.memset(gain_row[:], 0.0)
+        nc.sync.dma_start(out=gain_row[0:1, :], in_=scale1.unsqueeze(0))
+        eps = consts.tile([P, 1], F32)
+        nc.vector.memset(eps[:], EPS)
+        table_warm = consts.tile([P, 1], F32)
+        nc.scalar.activation(out=table_warm[:], in_=eps[:], func=ACT.Sqrt)
+
+        ident = consts.tile([P, P], F32)
+        make_identity(nc, ident[:])
+        ones = consts.tile([P, P], BF16)
+        nc.vector.memset(ones[:], 1.0)
+
+        x_tiles = []
+        for m in range(ROW_TILES):
+            x_sb = x_pool.tile([P, E], BF16)
+            nc.sync.dma_start(out=x_sb[:], in_=x_rows[m * P : (m + 1) * P, :])
+            x_tiles.append(x_sb)
+        w_raw = {}
+        for half in range(HALVES):
+            for g in range(PASSES):
+                w_sb = w_pool.tile([P, PACK, HALF_COLS], BF16)
+                nc.sync.dma_start(
+                    out=w_sb[:],
+                    in_=w_rows[
+                        g * K_PASS : (g + 1) * K_PASS, half * HALF_COLS : (half + 1) * HALF_COLS
+                    ].rearrange("(p t) n -> p t n", t=PACK),
+                )
+                w_raw[(half, g)] = w_sb
+
+        gain = consts.tile([P, E], BF16)
+        for j in range(E // N_BLOCK):
+            cols = slice(j * N_BLOCK, (j + 1) * N_BLOCK)
+            spread = psum.tile([P, N_BLOCK], F32, tag="bank")
+            nc.tensor.matmul(
+                out=spread[:], lhsT=ones[:], rhs=gain_row[:, cols], start=True, stop=True
+            )
+            nc.vector.tensor_copy(out=gain[:, cols], in_=spread[:])
+
+        x_codes = []
+        x_scales = []
+        for m in range(ROW_TILES):
+            x_sb = x_tiles[m]
+            squares = x_pool.tile([P, E], BF16)
+            sum_sq = x_pool.tile([P, 1], F32)
+            nc.scalar.activation(out=squares[:], in_=x_sb[:], func=ACT.Square, accum_out=sum_sq[:])
+            rms = x_pool.tile([P, 1], F32)
+            nc.scalar.activation(
+                out=rms[:], in_=sum_sq[:], func=ACT.Sqrt, scale=1.0 / E, bias=eps[:]
+            )
+            inv_rms = x_pool.tile([P, 1], F32)
+            nc.vector.reciprocal(out=inv_rms[:], in_=rms[:])
+            xn = x_pool.tile([P, E], BF16)
+            nc.vector.scalar_tensor_tensor(
+                out=xn[:], in0=x_sb[:], scalar=inv_rms[:], in1=gain[:], op0=ALU.mult, op1=ALU.mult
+            )
+            xn_words = xn[:].bitcast(F32)
+            x_grouped = x_pool.tile([P, PASSES, P, PACK], BF16, align_bytes=64)
+            for g in range(PASSES):
+                xt = psum.tile([P, PAIRS, P], F32, tag="bank")
+                for u in range(PAIRS):
+                    first = g * P * PAIRS + u
+                    nc.tensor.transpose(
+                        xt[:, u, :], xn_words[:, first : (g + 1) * P * PAIRS : PAIRS], ident[:]
+                    )
+                nc.scalar.copy(
+                    out=x_grouped[:, g, :, :]
+                    .rearrange("p r t -> p (r t)")
+                    .bitcast(F32)
+                    .rearrange("p (r u) -> p r u", u=PAIRS),
+                    in_=xt[:].rearrange("p u r -> p r u"),
+                )
+            codes = mx_pool.tile([P, PASSES, P], U32, name="x_codes%d" % m, align_bytes=64)
+            scales = mx_pool.tile([P, PASSES, P], U8, name="x_scales%d" % m, align_bytes=64)
+            nc.vector.quantize_mx(
+                out=codes[:].rearrange("p g r -> p (g r)").bitcast(FP8X4),
+                scales=scales[:].rearrange("p g r -> p (g r)"),
+                in_=x_grouped[:].rearrange("p g r t -> p (g r t)"),
+            )
+            x_codes.append(codes)
+            x_scales.append(scales)
+
+        units = [
+            (half, part, g)
+            for half in range(HALVES)
+            for part in range(PARTS)
+            for g in range(PASSES)
+        ]
+        w_grouped = {}
+        w_codes = {}
+        w_scales = {}
+        acc = {}
+
+        def regroup(unit):
+            half, part, g = unit
+            if part == PARTS - 1 and g == PASSES - 1:
+                grouped = stage.tile([P, N_BLOCK, PACK], BF16, name="by_scalar", align_bytes=64)
+                nc.scalar.copy(
+                    out=grouped[:].rearrange("p (h d) t -> p h d t", h=HEADS_PER_BLOCK),
+                    in_=w_raw[(half, g)][:].rearrange(
+                        "p t (h c d) -> p c h d t", h=HEADS_PER_BLOCK, c=PARTS
+                    )[:, part],
+                )
+            else:
+                grouped = stage.tile([P, N_BLOCK, PACK], BF16, name="by_vector", align_bytes=64)
+                nc.vector.tensor_copy(
+                    out=grouped[:].rearrange("p (h e i) t -> p h e t i", h=HEADS_PER_BLOCK, i=RUN),
+                    in_=w_raw[(half, g)][:].rearrange(
+                        "p t (h c e i) -> p c h e t i", h=HEADS_PER_BLOCK, c=PARTS, i=RUN
+                    )[:, part],
+                )
+            w_grouped[unit] = grouped
+
+        def quantise(unit):
+            codes = mx_pool.tile([P, N_BLOCK], U32, name="w_codes%d%d%d" % unit, align_bytes=64)
+            scales = mx_pool.tile([P, N_BLOCK], U8, name="w_scales%d%d%d" % unit, align_bytes=64)
+            nc.vector.quantize_mx(
+                out=codes[:].bitcast(FP8X4),
+                scales=scales[:],
+                in_=w_grouped[unit][:].rearrange("p n t -> p (n t)"),
+            )
+            w_codes[unit] = codes
+            w_scales[unit] = scales
+
+        def multiply(unit):
+            g = unit[2]
+            for m in range(ROW_TILES):
+                if g == 0:
+                    acc[m] = psum.tile([P, N_BLOCK], F32, name="acc", tag="bank")
+                nc.tensor.matmul_mx(
+                    out=acc[m][:],
+                    lhsT=x_codes[m][:, g, :].bitcast(FP8X4),
+                    lhsT_scale=x_scales[m][:, g, :],
+                    rhs=w_codes[unit][:].bitcast(FP8X4),
+                    rhs_scale=w_scales[unit][:],
+                    start=(g == 0),
+                    stop=(g == PASSES - 1),
+                )
+
+        def empty_and_store(unit):
+            half, part, g = unit
+            for m in range(ROW_TILES):
+                res = res_pool.tile([P, N_BLOCK], F32)
+                if unit == units[-1] and m % 2 == 1:
+                    nc.vector.tensor_copy(out=res[:], in_=acc[m][:])
+                else:
+                    nc.scalar.copy(out=res[:], in_=acc[m][:])
+                nc.sync.dma_start(
+                    out=out_rows[part][m * P : (m + 1) * P, half * N_BLOCK : (half + 1) * N_BLOCK],
+                    in_=res[:],
+                )
+
+        regroup(units[0])
+        for i, unit in enumerate(units):
+            if i + 1 < len(units):
+                regroup(units[i + 1])
+            quantise(unit)
+            multiply(unit)
+            if unit[2] == PASSES - 1:
+                empty_and_store(unit)

@@ -6,6 +6,7 @@ from concourse.masks import make_identity
 F32 = mybir.dt.float32
 BF16 = mybir.dt.bfloat16
 U32 = mybir.dt.uint32
+I32 = mybir.dt.int32
 U8 = mybir.dt.uint8
 FP8X4 = mybir.dt.float8_e4m3fn_x4
 ACT = mybir.ActivationFunctionType
@@ -21,15 +22,23 @@ E = 1024
 HEADS = 8
 D = 128
 PARTS = 3
+HEAD_COLS = PARTS * D
 EPS = 1e-6
 
 ROW_TILES = ROWS // P
 PASSES = E // K_PASS
-N_BLOCK = 512
-HEADS_PER_BLOCK = N_BLOCK // D
-HALVES = HEADS // HEADS_PER_BLOCK
-HALF_COLS = HEADS_PER_BLOCK * PARTS * D
 RUN = 4
+Q, K, V = range(PARTS)
+
+BLOCKS = [
+    [(0, 4, Q)],
+    [(0, 4, K)],
+    [(0, 4, V)],
+    [(4, 4, Q)],
+    [(4, 4, K)],
+    [(4, 4, V)],
+]
+W_LOADS = [(0, 4, 0), (0, 4, 1), (4, 4, 0), (4, 4, 1)]
 
 FLOPS = 2 * ROWS * E * HEADS * PARTS * D
 
@@ -41,171 +50,227 @@ def tile_block_pa_kernel(tc, x, scale1, w_qkv, out_0, out_1, out_2):
     out_rows = [o.rearrange("b s h d -> (b s) (h d)") for o in (out_0, out_1, out_2)]
 
     with ExitStack() as ctx:
-        consts = ctx.enter_context(tc.tile_pool(name="consts", bufs=1))
-        x_pool = ctx.enter_context(tc.tile_pool(name="x_pool", bufs=ROW_TILES))
-        w_pool = ctx.enter_context(tc.tile_pool(name="w_pool", bufs=PASSES * HALVES))
-        mx_pool = ctx.enter_context(tc.tile_pool(name="mx_pool", bufs=1))
-        stage = ctx.enter_context(tc.tile_pool(name="stage", bufs=3))
-        res_pool = ctx.enter_context(tc.tile_pool(name="res_pool", bufs=8))
+        keep = ctx.enter_context(tc.tile_pool(name="keep", bufs=1))
         psum = ctx.enter_context(tc.psum_pool(name="psum", bufs=8))
 
-        gain_row = consts.tile([P, E], BF16)
-        nc.vector.memset(gain_row[:], 0.0)
-        nc.sync.dma_start(out=gain_row[0:1, :], in_=scale1.unsqueeze(0))
-        eps = consts.tile([P, 1], F32)
-        nc.vector.memset(eps[:], EPS)
-        table_warm = consts.tile([P, 1], F32)
+        gain_row = keep.tile([P, E], BF16, name="gain_row")
+        nc.vector.memset(gain_row[:].bitcast(I32), 0)
+        eps = keep.tile([P, 1], F32, name="eps")
+        nc.vector.memset(eps[:], 0.0)
+        nc.vector.tensor_scalar_add(eps[:], eps[:], EPS)
+        table_warm = keep.tile([P, 1], F32, name="table_warm")
         nc.scalar.activation(out=table_warm[:], in_=eps[:], func=ACT.Sqrt)
-
-        ident = consts.tile([P, P], F32)
+        ones = keep.tile([P, P], BF16, name="ones")
+        nc.gpsimd.memset(ones[:], 1.0)
+        ident = keep.tile([P, P], F32, name="ident")
         make_identity(nc, ident[:])
-        ones = consts.tile([P, P], BF16)
-        nc.vector.memset(ones[:], 1.0)
 
-        x_tiles = []
-        for m in range(ROW_TILES):
-            x_sb = x_pool.tile([P, E], BF16)
-            nc.sync.dma_start(out=x_sb[:], in_=x_rows[m * P : (m + 1) * P, :])
-            x_tiles.append(x_sb)
-        w_raw = {}
-        for half in range(HALVES):
-            for g in range(PASSES):
-                w_sb = w_pool.tile([P, PACK, HALF_COLS], BF16)
-                nc.sync.dma_start(
-                    out=w_sb[:],
-                    in_=w_rows[
-                        g * K_PASS : (g + 1) * K_PASS, half * HALF_COLS : (half + 1) * HALF_COLS
-                    ].rearrange("(p t) n -> p t n", t=PACK),
-                )
-                w_raw[(half, g)] = w_sb
+        x_tiles = [keep.tile([P, E], BF16, name="x_sb%d" % m) for m in range(ROW_TILES)]
 
-        gain = consts.tile([P, E], BF16)
-        for j in range(E // N_BLOCK):
-            cols = slice(j * N_BLOCK, (j + 1) * N_BLOCK)
-            spread = psum.tile([P, N_BLOCK], F32, tag="bank")
-            nc.tensor.matmul(
-                out=spread[:], lhsT=ones[:], rhs=gain_row[:, cols], start=True, stop=True
+        def load_x(m):
+            nc.sync.dma_start(out=x_tiles[m][:], in_=x_rows[m * P : (m + 1) * P, :])
+
+        w_raw = []
+
+        def load_w(i):
+            head, heads, g = W_LOADS[i]
+            w_sb = keep.tile([P, PACK, heads * HEAD_COLS], BF16, name="w_sb%d" % i)
+            first = head * HEAD_COLS
+            nc.sync.dma_start(
+                out=w_sb[:],
+                in_=w_rows[
+                    g * K_PASS : (g + 1) * K_PASS, first : first + heads * HEAD_COLS
+                ].rearrange("(p t) n -> p t n", t=PACK),
             )
-            nc.vector.tensor_copy(out=gain[:, cols], in_=spread[:])
+            w_raw.append((head, heads, g, w_sb))
 
-        x_codes = []
-        x_scales = []
-        for m in range(ROW_TILES):
-            x_sb = x_tiles[m]
-            squares = x_pool.tile([P, E], BF16)
-            sum_sq = x_pool.tile([P, 1], F32)
-            nc.scalar.activation(out=squares[:], in_=x_sb[:], func=ACT.Square, accum_out=sum_sq[:])
-            rms = x_pool.tile([P, 1], F32)
+        load_x(0)
+        nc.sync.dma_start(out=gain_row[0:1, :], in_=scale1.unsqueeze(0))
+        load_x(1)
+        load_x(2)
+        load_x(3)
+        for i in range(len(W_LOADS)):
+            load_w(i)
+
+        sum_sq = keep.tile([P, ROW_TILES], F32, name="sum_sq")
+        rms = keep.tile([P, ROW_TILES], F32, name="rms")
+        inv_rms = keep.tile([P, ROW_TILES], F32, name="inv_rms")
+        gain = keep.tile([P, E], BF16, name="gain")
+        x_codes = {}
+        x_scales = {}
+        xn_tiles = {}
+        xt_banks = {}
+        x_grouped = {}
+
+        def square(m):
+            squares = keep.tile([P, E], BF16, name="squares%d" % m)
             nc.scalar.activation(
-                out=rms[:], in_=sum_sq[:], func=ACT.Sqrt, scale=1.0 / E, bias=eps[:]
+                out=squares[:], in_=x_tiles[m][:], func=ACT.Square, accum_out=sum_sq[:, m : m + 1]
             )
-            inv_rms = x_pool.tile([P, 1], F32)
-            nc.vector.reciprocal(out=inv_rms[:], in_=rms[:])
-            xn = x_pool.tile([P, E], BF16)
+
+        def square_vector(m):
+            squares = keep.tile([P, E], BF16, name="squares%d" % m)
             nc.vector.scalar_tensor_tensor(
-                out=xn[:], in0=x_sb[:], scalar=inv_rms[:], in1=gain[:], op0=ALU.mult, op1=ALU.mult
+                out=squares[:], in0=x_tiles[m][:], scalar=1.0, in1=x_tiles[m][:],
+                op0=ALU.mult, op1=ALU.mult, accum_out=sum_sq[:, m : m + 1],
             )
-            xn_words = xn[:].bitcast(F32)
-            x_grouped = x_pool.tile([P, PASSES, P, PACK], BF16, align_bytes=64)
+
+        def root(first, last):
+            nc.scalar.activation(
+                out=rms[:, first:last], in_=sum_sq[:, first:last], func=ACT.Sqrt,
+                scale=1.0 / E, bias=eps[:],
+            )
+            nc.vector.reciprocal(out=inv_rms[:, first:last], in_=rms[:, first:last])
+
+        def spread_gain():
+            spread = psum.tile([P, E], BF16, name="spread", tag="bank")
+            for j in range(2):
+                cols = slice(j * E // 2, (j + 1) * E // 2)
+                nc.tensor.matmul(
+                    out=spread[:, cols], lhsT=ones[:], rhs=gain_row[:, cols], start=True, stop=True
+                )
+            nc.vector.tensor_copy(out=gain[:], in_=spread[:])
+
+        def normalise(m):
+            xn = keep.tile([P, E], BF16, name="xn%d" % m)
+            nc.vector.scalar_tensor_tensor(
+                out=xn[:], in0=x_tiles[m][:], scalar=inv_rms[:, m : m + 1], in1=gain[:],
+                op0=ALU.mult, op1=ALU.mult,
+            )
+            xn_tiles[m] = xn
+
+        def transpose_x(m):
+            words = xn_tiles[m][:].bitcast(F32)
+            xt = psum.tile([P, PASSES, PAIRS, P], F32, name="xt%d" % m, tag="bank")
             for g in range(PASSES):
-                xt = psum.tile([P, PAIRS, P], F32, tag="bank")
                 for u in range(PAIRS):
                     first = g * P * PAIRS + u
                     nc.tensor.transpose(
-                        xt[:, u, :], xn_words[:, first : (g + 1) * P * PAIRS : PAIRS], ident[:]
+                        xt[:, g, u, :], words[:, first : (g + 1) * P * PAIRS : PAIRS], ident[:]
                     )
-                nc.scalar.copy(
-                    out=x_grouped[:, g, :, :]
-                    .rearrange("p r t -> p (r t)")
-                    .bitcast(F32)
-                    .rearrange("p (r u) -> p r u", u=PAIRS),
-                    in_=xt[:].rearrange("p u r -> p r u"),
-                )
-            codes = mx_pool.tile([P, PASSES, P], U32, name="x_codes%d" % m, align_bytes=64)
-            scales = mx_pool.tile([P, PASSES, P], U8, name="x_scales%d" % m, align_bytes=64)
+            xt_banks[m] = xt
+
+        def regroup_x(m):
+            grouped = keep.tile([P, PASSES, P, PACK], BF16, name="x_grouped%d" % m, align_bytes=64)
+            nc.scalar.copy(
+                out=grouped[:]
+                .rearrange("p g r t -> p (g r t)")
+                .bitcast(F32)
+                .rearrange("p (g r u) -> p g r u", g=PASSES, u=PAIRS),
+                in_=xt_banks[m][:].rearrange("p g u r -> p g r u"),
+            )
+            x_grouped[m] = grouped
+
+        def quantise_x(m):
+            codes = keep.tile([P, PASSES, P], U32, name="x_codes%d" % m, align_bytes=64)
+            scales = keep.tile([P, PASSES, P], U8, name="x_scales%d" % m, align_bytes=64)
             nc.vector.quantize_mx(
                 out=codes[:].rearrange("p g r -> p (g r)").bitcast(FP8X4),
                 scales=scales[:].rearrange("p g r -> p (g r)"),
-                in_=x_grouped[:].rearrange("p g r t -> p (g r t)"),
+                in_=x_grouped[m][:].rearrange("p g r t -> p (g r t)"),
             )
-            x_codes.append(codes)
-            x_scales.append(scales)
+            x_codes[m] = codes
+            x_scales[m] = scales
 
-        units = [
-            (half, part, g)
-            for half in range(HALVES)
-            for part in range(PARTS)
-            for g in range(PASSES)
-        ]
         w_grouped = {}
         w_codes = {}
         w_scales = {}
         acc = {}
 
-        def regroup(unit):
-            half, part, g = unit
-            if part == PARTS - 1 and g == PASSES - 1:
-                grouped = stage.tile([P, N_BLOCK, PACK], BF16, name="by_scalar", align_bytes=64)
-                nc.scalar.copy(
-                    out=grouped[:].rearrange("p (h d) t -> p h d t", h=HEADS_PER_BLOCK),
-                    in_=w_raw[(half, g)][:].rearrange(
-                        "p t (h c d) -> p c h d t", h=HEADS_PER_BLOCK, c=PARTS
-                    )[:, part],
-                )
-            else:
-                grouped = stage.tile([P, N_BLOCK, PACK], BF16, name="by_vector", align_bytes=64)
-                nc.vector.tensor_copy(
-                    out=grouped[:].rearrange("p (h e i) t -> p h e t i", h=HEADS_PER_BLOCK, i=RUN),
-                    in_=w_raw[(half, g)][:].rearrange(
-                        "p t (h c e i) -> p c h e t i", h=HEADS_PER_BLOCK, c=PARTS, i=RUN
-                    )[:, part],
-                )
-            w_grouped[unit] = grouped
+        def width(b):
+            return D * sum(heads for head, heads, part in BLOCKS[b])
 
-        def quantise(unit):
-            codes = mx_pool.tile([P, N_BLOCK], U32, name="w_codes%d%d%d" % unit, align_bytes=64)
-            scales = mx_pool.tile([P, N_BLOCK], U8, name="w_scales%d%d%d" % unit, align_bytes=64)
+        def regroup(b, g, by="vector", head_range=(0, HEADS)):
+            if (b, g) not in w_grouped:
+                w_grouped[(b, g)] = keep.tile(
+                    [P, width(b), PACK], BF16, name="w_grouped%d_%d" % (b, g), align_bytes=64
+                )
+            column = 0
+            for head, heads, part in BLOCKS[b]:
+                for w_head, w_heads, w_g, w_sb in w_raw:
+                    low = max(head, w_head, head_range[0])
+                    high = min(head + heads, w_head + w_heads, head_range[1])
+                    if w_g != g or low >= high:
+                        continue
+                    count = high - low
+                    first = column + (low - head) * D
+                    out = w_grouped[(b, g)][:, first : first + count * D, :]
+                    source = w_sb[:, :, (low - w_head) * HEAD_COLS : (high - w_head) * HEAD_COLS]
+                    if by == "vector":
+                        nc.vector.tensor_copy(
+                            out=out.rearrange("p (h e i) t -> p h e t i", h=count, i=RUN),
+                            in_=source.rearrange(
+                                "p t (h c e i) -> p c h e t i", h=count, c=PARTS, i=RUN
+                            )[:, part],
+                        )
+                    elif by == "scalar":
+                        nc.scalar.copy(
+                            out=out.rearrange("p (h d) t -> p h d t", h=count),
+                            in_=source.rearrange("p t (h c d) -> p c h d t", h=count, c=PARTS)[:, part],
+                        )
+                column += heads * D
+
+        def quantise(b, g):
+            codes = keep.tile([P, width(b)], U32, name="w_codes%d_%d" % (b, g), align_bytes=64)
+            scales = keep.tile([P, width(b)], U8, name="w_scales%d_%d" % (b, g), align_bytes=64)
             nc.vector.quantize_mx(
                 out=codes[:].bitcast(FP8X4),
                 scales=scales[:],
-                in_=w_grouped[unit][:].rearrange("p n t -> p (n t)"),
+                in_=w_grouped[(b, g)][:].rearrange("p n t -> p (n t)"),
             )
-            w_codes[unit] = codes
-            w_scales[unit] = scales
+            w_codes[(b, g)] = codes
+            w_scales[(b, g)] = scales
 
-        def multiply(unit):
-            g = unit[2]
-            for m in range(ROW_TILES):
-                if g == 0:
-                    acc[m] = psum.tile([P, N_BLOCK], F32, name="acc", tag="bank")
-                nc.tensor.matmul_mx(
-                    out=acc[m][:],
-                    lhsT=x_codes[m][:, g, :].bitcast(FP8X4),
-                    lhsT_scale=x_scales[m][:, g, :],
-                    rhs=w_codes[unit][:].bitcast(FP8X4),
-                    rhs_scale=w_scales[unit][:],
-                    start=(g == 0),
-                    stop=(g == PASSES - 1),
-                )
+        def multiply(b, m, g):
+            if g == 0:
+                acc[(b, m)] = psum.tile([P, width(b)], F32, name="acc", tag="bank")
+            nc.tensor.matmul_mx(
+                out=acc[(b, m)][:],
+                lhsT=x_codes[m][:, g, :].bitcast(FP8X4),
+                lhsT_scale=x_scales[m][:, g, :],
+                rhs=w_codes[(b, g)][:].bitcast(FP8X4),
+                rhs_scale=w_scales[(b, g)][:],
+                start=(g == 0),
+                stop=(g == PASSES - 1),
+            )
 
-        def empty_and_store(unit):
-            half, part, g = unit
-            for m in range(ROW_TILES):
-                res = res_pool.tile([P, N_BLOCK], F32)
-                if unit == units[-1] and m % 2 == 1:
-                    nc.vector.tensor_copy(out=res[:], in_=acc[m][:])
-                else:
-                    nc.scalar.copy(out=res[:], in_=acc[m][:])
+        def empty(b, m, by="scalar"):
+            res = keep.tile([P, width(b)], F32, name="res%d_%d" % (b, m))
+            if by == "vector":
+                nc.vector.tensor_copy(out=res[:], in_=acc[(b, m)][:])
+            else:
+                nc.scalar.copy(out=res[:], in_=acc[(b, m)][:])
+            column = 0
+            for head, heads, part in BLOCKS[b]:
                 nc.sync.dma_start(
-                    out=out_rows[part][m * P : (m + 1) * P, half * N_BLOCK : (half + 1) * N_BLOCK],
-                    in_=res[:],
+                    out=out_rows[part][m * P : (m + 1) * P, head * D : (head + heads) * D],
+                    in_=res[:, column : column + heads * D],
                 )
+                column += heads * D
 
-        regroup(units[0])
-        for i, unit in enumerate(units):
-            if i + 1 < len(units):
-                regroup(units[i + 1])
-            quantise(unit)
-            multiply(unit)
-            if unit[2] == PASSES - 1:
-                empty_and_store(unit)
+
+        for m in range(ROW_TILES):
+            square(m)
+            root(m, m + 1)
+            if m == 0:
+                spread_gain()
+            normalise(m)
+            transpose_x(m)
+            regroup_x(m)
+            quantise_x(m)
+        regroup(0, 0)
+        by_scalar = [(1, 0), (2, 1), (4, 0)]
+        order = [(b, g) for b in range(len(BLOCKS)) for g in range(PASSES)]
+        ahead = list(by_scalar)
+        for i, (b, g) in enumerate(order):
+            while ahead and order.index(ahead[0]) <= i + 4:
+                regroup(*ahead[0], by="scalar")
+                ahead.remove(ahead[0])
+            if i + 1 < len(order) and order[i + 1] not in by_scalar:
+                regroup(*order[i + 1])
+            quantise(b, g)
+            for m in range(ROW_TILES):
+                multiply(b, m, g)
+            if g == PASSES - 1:
+                for m in range(ROW_TILES):
+                    empty(b, m, by="vector" if b == len(BLOCKS) - 1 and m % 2 == 0 else "scalar")

@@ -28,6 +28,7 @@ EPS = 1e-6
 ROW_TILES = ROWS // P
 PASSES = E // K_PASS
 RUN = 4
+N_BLOCK = 512
 Q, K, V = range(PARTS)
 
 BLOCKS = [
@@ -52,6 +53,7 @@ def tile_block_pa_kernel(tc, x, scale1, w_qkv, out_0, out_1, out_2):
     with ExitStack() as ctx:
         keep = ctx.enter_context(tc.tile_pool(name="keep", bufs=1))
         psum = ctx.enter_context(tc.psum_pool(name="psum", bufs=8))
+        ctx.enter_context(tc.manual_schedule())
 
         gain_row = keep.tile([P, E], BF16, name="gain_row")
         nc.vector.memset(gain_row[:].bitcast(I32), 0)
@@ -59,7 +61,7 @@ def tile_block_pa_kernel(tc, x, scale1, w_qkv, out_0, out_1, out_2):
         nc.vector.memset(eps[:], 0.0)
         nc.vector.tensor_scalar_add(eps[:], eps[:], EPS)
         table_warm = keep.tile([P, 1], F32, name="table_warm")
-        nc.scalar.activation(out=table_warm[:], in_=eps[:], func=ACT.Sqrt)
+        nc.scalar.activation(out=table_warm[:], in_=eps[:], func=ACT.Abs_reciprocal_sqrt)
         ones = keep.tile([P, P], BF16, name="ones")
         nc.gpsimd.memset(ones[:], 1.0)
         ident = keep.tile([P, P], F32, name="ident")
@@ -89,11 +91,12 @@ def tile_block_pa_kernel(tc, x, scale1, w_qkv, out_0, out_1, out_2):
         load_x(1)
         load_x(2)
         load_x(3)
-        for i in range(len(W_LOADS)):
-            load_w(i)
+        load_w(0)
+        load_w(1)
+        load_w(2)
+        load_w(3)
 
         sum_sq = keep.tile([P, ROW_TILES], F32, name="sum_sq")
-        rms = keep.tile([P, ROW_TILES], F32, name="rms")
         inv_rms = keep.tile([P, ROW_TILES], F32, name="inv_rms")
         gain = keep.tile([P, E], BF16, name="gain")
         x_codes = {}
@@ -117,10 +120,9 @@ def tile_block_pa_kernel(tc, x, scale1, w_qkv, out_0, out_1, out_2):
 
         def root(first, last):
             nc.scalar.activation(
-                out=rms[:, first:last], in_=sum_sq[:, first:last], func=ACT.Sqrt,
+                out=inv_rms[:, first:last], in_=sum_sq[:, first:last], func=ACT.Abs_reciprocal_sqrt,
                 scale=1.0 / E, bias=eps[:],
             )
-            nc.vector.reciprocal(out=inv_rms[:, first:last], in_=rms[:, first:last])
 
         def spread_gain():
             spread = psum.tile([P, E], BF16, name="spread", tag="bank")
@@ -205,31 +207,36 @@ def tile_block_pa_kernel(tc, x, scale1, w_qkv, out_0, out_1, out_2):
                         )
                     elif by == "scalar":
                         nc.scalar.copy(
-                            out=out.rearrange("p (h d) t -> p h d t", h=count),
-                            in_=source.rearrange("p t (h c d) -> p c h d t", h=count, c=PARTS)[:, part],
+                            out=out.rearrange("p (h e i) t -> p h e t i", h=count, i=RUN),
+                            in_=source.rearrange(
+                                "p t (h c e i) -> p c h e t i", h=count, c=PARTS, i=RUN
+                            )[:, part],
                         )
                 column += heads * D
 
-        def quantise(b, g):
-            codes = keep.tile([P, width(b)], U32, name="w_codes%d_%d" % (b, g), align_bytes=64)
-            scales = keep.tile([P, width(b)], U8, name="w_scales%d_%d" % (b, g), align_bytes=64)
+        def quantise(b, g, cols=slice(0, N_BLOCK)):
+            if (b, g) not in w_codes:
+                w_codes[(b, g)] = keep.tile(
+                    [P, width(b)], U32, name="w_codes%d_%d" % (b, g), align_bytes=64
+                )
+                w_scales[(b, g)] = keep.tile(
+                    [P, width(b)], U8, name="w_scales%d_%d" % (b, g), align_bytes=64
+                )
             nc.vector.quantize_mx(
-                out=codes[:].bitcast(FP8X4),
-                scales=scales[:],
-                in_=w_grouped[(b, g)][:].rearrange("p n t -> p (n t)"),
+                out=w_codes[(b, g)][:, cols].bitcast(FP8X4),
+                scales=w_scales[(b, g)][:, cols],
+                in_=w_grouped[(b, g)][:, cols, :].rearrange("p n t -> p (n t)"),
             )
-            w_codes[(b, g)] = codes
-            w_scales[(b, g)] = scales
 
-        def multiply(b, m, g):
-            if g == 0:
+        def multiply(b, m, g, cols=slice(0, N_BLOCK)):
+            if (b, m) not in acc:
                 acc[(b, m)] = psum.tile([P, width(b)], F32, name="acc", tag="bank")
             nc.tensor.matmul_mx(
-                out=acc[(b, m)][:],
+                out=acc[(b, m)][:, cols],
                 lhsT=x_codes[m][:, g, :].bitcast(FP8X4),
                 lhsT_scale=x_scales[m][:, g, :],
-                rhs=w_codes[(b, g)][:].bitcast(FP8X4),
-                rhs_scale=w_scales[(b, g)][:],
+                rhs=w_codes[(b, g)][:, cols].bitcast(FP8X4),
+                rhs_scale=w_scales[(b, g)][:, cols],
                 start=(g == 0),
                 stop=(g == PASSES - 1),
             )
@@ -248,29 +255,81 @@ def tile_block_pa_kernel(tc, x, scale1, w_qkv, out_0, out_1, out_2):
                 )
                 column += heads * D
 
-
-        for m in range(ROW_TILES):
-            square(m)
-            root(m, m + 1)
-            if m == 0:
-                spread_gain()
-            normalise(m)
-            transpose_x(m)
-            regroup_x(m)
-            quantise_x(m)
-        regroup(0, 0)
-        by_scalar = [(1, 0), (2, 1), (4, 0)]
-        order = [(b, g) for b in range(len(BLOCKS)) for g in range(PASSES)]
-        ahead = list(by_scalar)
-        for i, (b, g) in enumerate(order):
-            while ahead and order.index(ahead[0]) <= i + 4:
-                regroup(*ahead[0], by="scalar")
-                ahead.remove(ahead[0])
-            if i + 1 < len(order) and order[i + 1] not in by_scalar:
-                regroup(*order[i + 1])
-            quantise(b, g)
+        def multiply_all(b, g, cols=slice(0, N_BLOCK)):
             for m in range(ROW_TILES):
-                multiply(b, m, g)
-            if g == PASSES - 1:
-                for m in range(ROW_TILES):
-                    empty(b, m, by="vector" if b == len(BLOCKS) - 1 and m % 2 == 0 else "scalar")
+                multiply(b, m, g, cols)
+
+        def empty_all(b, shared=False):
+            for m in range(ROW_TILES):
+                empty(b, m, by="vector" if shared and m % 2 == 0 else "scalar")
+
+        square(0)
+        square_vector(1)
+        root(0, 1)
+        spread_gain()
+        square(2)
+        normalise(0)
+        transpose_x(0)
+        root(1, 2)
+        square(3)
+        normalise(1)
+        transpose_x(1)
+        root(2, 3)
+        normalise(2)
+        root(3, 4)
+        normalise(3)
+        transpose_x(2)
+        transpose_x(3)
+        regroup_x(0)
+        regroup_x(1)
+        regroup(1, 0, by="scalar", head_range=(0, 2))
+        regroup_x(2)
+        regroup_x(3)
+        regroup(0, 0)
+        quantise_x(0)
+        quantise_x(1)
+        quantise(0, 0)
+        quantise_x(2)
+        quantise_x(3)
+        multiply_all(0, 0)
+        regroup(1, 0, by="scalar", head_range=(2, 4))
+        regroup(0, 1)
+        quantise(1, 0)
+        quantise(0, 1)
+        multiply_all(0, 1)
+        regroup(1, 1, by="scalar")
+        regroup(2, 0)
+        regroup(4, 0, by="scalar", head_range=(4, 6))
+        empty_all(0)
+        multiply_all(1, 0)
+        quantise(1, 1)
+        multiply_all(1, 1)
+        regroup(2, 1)
+        regroup(5, 0, by="scalar", head_range=(4, 6))
+        empty_all(1)
+        quantise(2, 0)
+        multiply_all(2, 0)
+        regroup(3, 0)
+        quantise(2, 1)
+        multiply_all(2, 1)
+        empty_all(2)
+        regroup(3, 1)
+        quantise(3, 0)
+        multiply_all(3, 0)
+        regroup(4, 0, head_range=(6, 8))
+        quantise(3, 1)
+        multiply_all(3, 1)
+        empty_all(3)
+        regroup(4, 1)
+        quantise(4, 0)
+        multiply_all(4, 0)
+        regroup(5, 0, head_range=(6, 8))
+        quantise(4, 1)
+        multiply_all(4, 1)
+        empty_all(4)
+        quantise(5, 0)
+        multiply_all(5, 0)
+        regroup(5, 1)
+        quantise(5, 1)
+        multiply_all(5, 1)
+        empty_all(5, shared=True)

@@ -98,7 +98,7 @@ def tile_block_pa_kernel(tc, x, scale1, w_qkv, out_0, out_1, out_2):
 
         sum_sq = keep.tile([P, ROW_TILES], F32, name="sum_sq")
         inv_rms = keep.tile([P, ROW_TILES], F32, name="inv_rms")
-        gain = keep.tile([P, E], BF16, name="gain")
+        gain = []
         x_codes = {}
         x_scales = {}
         xn_tiles = {}
@@ -131,12 +131,12 @@ def tile_block_pa_kernel(tc, x, scale1, w_qkv, out_0, out_1, out_2):
                 nc.tensor.matmul(
                     out=spread[:, cols], lhsT=ones[:], rhs=gain_row[:, cols], start=True, stop=True
                 )
-            nc.vector.tensor_copy(out=gain[:], in_=spread[:])
+            gain.append(spread)
 
         def normalise(m):
             xn = keep.tile([P, E], BF16, name="xn%d" % m)
             nc.vector.scalar_tensor_tensor(
-                out=xn[:], in0=x_tiles[m][:], scalar=inv_rms[:, m : m + 1], in1=gain[:],
+                out=xn[:], in0=x_tiles[m][:], scalar=inv_rms[:, m : m + 1], in1=gain[0][:],
                 op0=ALU.mult, op1=ALU.mult,
             )
             xn_tiles[m] = xn
@@ -299,20 +299,20 @@ def tile_block_pa_kernel(tc, x, scale1, w_qkv, out_0, out_1, out_2):
         multiply_all(0, 1)
         regroup(1, 1, by="scalar")
         regroup(2, 0)
-        regroup(4, 0, by="scalar", head_range=(4, 6))
         empty_all(0)
         multiply_all(1, 0)
         quantise(1, 1)
         multiply_all(1, 1)
         regroup(2, 1)
-        regroup(5, 0, by="scalar", head_range=(4, 6))
         empty_all(1)
+        regroup(4, 0, by="scalar", head_range=(4, 6))
         quantise(2, 0)
         multiply_all(2, 0)
         regroup(3, 0)
         quantise(2, 1)
         multiply_all(2, 1)
         empty_all(2)
+        regroup(5, 0, by="scalar", head_range=(4, 6))
         regroup(3, 1)
         quantise(3, 0)
         multiply_all(3, 0)

@@ -56,7 +56,7 @@ def tile_block_pa_kernel(tc, x, scale1, w_qkv, out_0, out_1, out_2):
         ctx.enter_context(tc.manual_schedule())
 
         gain_row = keep.tile([P, E], BF16, name="gain_row")
-        nc.vector.memset(gain_row[:].bitcast(I32), 0)
+        nc.gpsimd.memset(gain_row[:].bitcast(I32), 0)
         eps = keep.tile([P, 1], F32, name="eps")
         nc.vector.memset(eps[:], 0.0)
         nc.vector.tensor_scalar_add(eps[:], eps[:], EPS)
@@ -298,7 +298,8 @@ def tile_block_pa_kernel(tc, x, scale1, w_qkv, out_0, out_1, out_2):
         quantise(0, 1)
         multiply_all(0, 1)
         regroup(1, 1, by="scalar")
-        regroup(2, 0)
+        regroup(2, 0, by="scalar", head_range=(0, 2))
+        regroup(2, 0, head_range=(2, 4))
         empty_all(0)
         multiply_all(1, 0)
         quantise(1, 1)

@@ -27,7 +27,7 @@ EPS = 1e-6
 
 ROW_TILES = ROWS // P
 PASSES = E // K_PASS
-RUN = 4
+RUN = 8
 N_BLOCK = 512
 Q, K, V = range(PARTS)
 

@@ -263,6 +263,14 @@ def tile_block_pa_kernel(tc, x, scale1, w_qkv, out_0, out_1, out_2):
             for m in range(ROW_TILES):
                 empty(b, m, by="vector" if shared and m % 2 == 0 else "scalar")
 
+        warm = psum.tile([P, N_BLOCK], F32, name="warm", tag="bank")
+
+        def keep_warm(times):
+            for i in range(times):
+                nc.tensor.matmul(
+                    out=warm[:], lhsT=ones[:], rhs=gain_row[:, :N_BLOCK], start=True, stop=True
+                )
+
         square(0)
         square_vector(1)
         root(0, 1)
@@ -291,7 +299,9 @@ def tile_block_pa_kernel(tc, x, scale1, w_qkv, out_0, out_1, out_2):
         quantise(0, 0)
         quantise_x(2)
         quantise_x(3)
+        keep_warm(4)
         multiply_all(0, 0)
+        keep_warm(3)
         regroup(1, 0, by="scalar", head_range=(2, 4))
         regroup(0, 1)
         quantise(1, 0)
@@ -299,11 +309,11 @@ def tile_block_pa_kernel(tc, x, scale1, w_qkv, out_0, out_1, out_2):
         multiply_all(0, 1)
         regroup(1, 1, by="scalar")
         regroup(2, 0, by="scalar", head_range=(0, 2))
-        regroup(2, 0, head_range=(2, 4))
         empty_all(0)
         multiply_all(1, 0)
         quantise(1, 1)
         multiply_all(1, 1)
+        regroup(2, 0, head_range=(2, 4))
         regroup(2, 1)
         empty_all(1)
         regroup(4, 0, by="scalar", head_range=(4, 6))

from contextlib import ExitStack

import concourse.mybir as mybir
from concourse.masks import make_identity

F32 = mybir.dt.float32
BF16 = mybir.dt.bfloat16
U32 = mybir.dt.uint32
I32 = mybir.dt.int32
U8 = mybir.dt.uint8
FP8X4 = mybir.dt.float8_e4m3fn_x4
ACT = mybir.ActivationFunctionType
ALU = mybir.AluOpType

P = 128
PACK = 4
PAIRS = PACK // 2
K_PASS = P * PACK

ROWS = 512
E = 1024
HEADS = 8
D = 128
PARTS = 3
HEAD_COLS = PARTS * D
EPS = 1e-6

ROW_TILES = ROWS // P
PASSES = E // K_PASS
RUN = 8
N_BLOCK = 512
Q, K, V = range(PARTS)

BLOCKS = [
    [(0, 4, Q)],
    [(0, 4, K)],
    [(0, 4, V)],
    [(4, 4, Q)],
    [(4, 4, K)],
    [(4, 4, V)],
]
W_LOADS = [(0, 4, 0), (0, 4, 1), (4, 4, 0), (4, 4, 1)]

FLOPS = 2 * ROWS * E * HEADS * PARTS * D


def tile_block_pa_kernel(tc, x, scale1, w_qkv, out_0, out_1, out_2):
    nc = tc.nc
    x_rows = x.rearrange("b s e -> (b s) e")
    w_rows = w_qkv.rearrange("e h c -> e (h c)")
    out_rows = [o.rearrange("b s h d -> (b s) (h d)") for o in (out_0, out_1, out_2)]

    with ExitStack() as ctx:
        keep = ctx.enter_context(tc.tile_pool(name="keep", bufs=1))
        psum = ctx.enter_context(tc.psum_pool(name="psum", bufs=8))
        ctx.enter_context(tc.manual_schedule())

        gain_row = keep.tile([P, E], BF16, name="gain_row")
        nc.gpsimd.memset(gain_row[:].bitcast(I32), 0)
        eps = keep.tile([P, 1], F32, name="eps")
        nc.vector.memset(eps[:], 0.0)
        nc.vector.tensor_scalar_add(eps[:], eps[:], EPS)
        table_warm = keep.tile([P, 1], F32, name="table_warm")
        nc.scalar.activation(out=table_warm[:], in_=eps[:], func=ACT.Abs_reciprocal_sqrt)
        ones = keep.tile([P, P], BF16, name="ones")
        nc.gpsimd.memset(ones[:], 1.0)
        ident = keep.tile([P, P], F32, name="ident")
        make_identity(nc, ident[:])

        x_tiles = [keep.tile([P, E], BF16, name="x_sb%d" % m) for m in range(ROW_TILES)]

        def load_x(m):
            nc.sync.dma_start(out=x_tiles[m][:], in_=x_rows[m * P : (m + 1) * P, :])

        w_raw = []

        def load_w(i):
            head, heads, g = W_LOADS[i]
            w_sb = keep.tile([P, PACK, heads * HEAD_COLS], BF16, name="w_sb%d" % i)
            first = head * HEAD_COLS
            nc.sync.dma_start(
                out=w_sb[:],
                in_=w_rows[
                    g * K_PASS : (g + 1) * K_PASS, first : first + heads * HEAD_COLS
                ].rearrange("(p t) n -> p t n", t=PACK),
            )
            w_raw.append((head, heads, g, w_sb))

        load_x(0)
        nc.sync.dma_start(out=gain_row[0:1, :], in_=scale1.unsqueeze(0))
        load_x(1)
        load_x(2)
        load_x(3)
        load_w(0)
        load_w(1)
        load_w(2)
        load_w(3)

        sum_sq = keep.tile([P, ROW_TILES], F32, name="sum_sq")
        inv_rms = keep.tile([P, ROW_TILES], F32, name="inv_rms")
        gain = []
        x_codes = {}
        x_scales = {}
        xn_tiles = {}
        xt_banks = {}
        x_grouped = {}

        def square(m):
            squares = keep.tile([P, E], BF16, name="squares%d" % m)
            nc.scalar.activation(
                out=squares[:], in_=x_tiles[m][:], func=ACT.Square, accum_out=sum_sq[:, m : m + 1]
            )

        def square_vector(m):
            squares = keep.tile([P, E], BF16, name="squares%d" % m)
            nc.vector.scalar_tensor_tensor(
                out=squares[:], in0=x_tiles[m][:], scalar=1.0, in1=x_tiles[m][:],
                op0=ALU.mult, op1=ALU.mult, accum_out=sum_sq[:, m : m + 1],
            )

        def root(first, last):
            nc.scalar.activation(
                out=inv_rms[:, first:last], in_=sum_sq[:, first:last], func=ACT.Abs_reciprocal_sqrt,
                scale=1.0 / E, bias=eps[:],
            )

        def spread_gain():
            spread = psum.tile([P, E], BF16, name="spread", tag="bank")
            for j in range(2):
                cols = slice(j * E // 2, (j + 1) * E // 2)
                nc.tensor.matmul(
                    out=spread[:, cols], lhsT=ones[:], rhs=gain_row[:, cols], start=True, stop=True
                )
            gain.append(spread)

        def normalise(m):
            xn = keep.tile([P, E], BF16, name="xn%d" % m)
            nc.vector.scalar_tensor_tensor(
                out=xn[:], in0=x_tiles[m][:], scalar=inv_rms[:, m : m + 1], in1=gain[0][:],
                op0=ALU.mult, op1=ALU.mult,
            )
            xn_tiles[m] = xn

        def transpose_x(m):
            words = xn_tiles[m][:].bitcast(F32)
            xt = psum.tile([P, PASSES, PAIRS, P], F32, name="xt%d" % m, tag="bank")
            for g in range(PASSES):
                for u in range(PAIRS):
                    first = g * P * PAIRS + u
                    nc.tensor.transpose(
                        xt[:, g, u, :], words[:, first : (g + 1) * P * PAIRS : PAIRS], ident[:]
                    )
            xt_banks[m] = xt

        def regroup_x(m):
            grouped = keep.tile([P, PASSES, P, PACK], BF16, name="x_grouped%d" % m, align_bytes=64)
            nc.scalar.copy(
                out=grouped[:]
                .rearrange("p g r t -> p (g r t)")
                .bitcast(F32)
                .rearrange("p (g r u) -> p g r u", g=PASSES, u=PAIRS),
                in_=xt_banks[m][:].rearrange("p g u r -> p g r u"),
            )
            x_grouped[m] = grouped

        def quantise_x(m):
            codes = keep.tile([P, PASSES, P], U32, name="x_codes%d" % m, align_bytes=64)
            scales = keep.tile([P, PASSES, P], U8, name="x_scales%d" % m, align_bytes=64)
            nc.vector.quantize_mx(
                out=codes[:].rearrange("p g r -> p (g r)").bitcast(FP8X4),
                scales=scales[:].rearrange("p g r -> p (g r)"),
                in_=x_grouped[m][:].rearrange("p g r t -> p (g r t)"),
            )
            x_codes[m] = codes
            x_scales[m] = scales

        w_grouped = {}
        w_codes = {}
        w_scales = {}
        acc = {}

        def width(b):
            return D * sum(heads for head, heads, part in BLOCKS[b])

        def regroup(b, g, by="vector", head_range=(0, HEADS)):
            if (b, g) not in w_grouped:
                w_grouped[(b, g)] = keep.tile(
                    [P, width(b), PACK], BF16, name="w_grouped%d_%d" % (b, g), align_bytes=64
                )
            column = 0
            for head, heads, part in BLOCKS[b]:
                for w_head, w_heads, w_g, w_sb in w_raw:
                    low = max(head, w_head, head_range[0])
                    high = min(head + heads, w_head + w_heads, head_range[1])
                    if w_g != g or low >= high:
                        continue
                    count = high - low
                    first = column + (low - head) * D
                    out = w_grouped[(b, g)][:, first : first + count * D, :]
                    source = w_sb[:, :, (low - w_head) * HEAD_COLS : (high - w_head) * HEAD_COLS]
                    if by == "vector":
                        nc.vector.tensor_copy(
                            out=out.rearrange("p (h e i) t -> p h e t i", h=count, i=RUN),
                            in_=source.rearrange(
                                "p t (h c e i) -> p c h e t i", h=count, c=PARTS, i=RUN
                            )[:, part],
                        )
                    elif by == "scalar":
                        nc.scalar.copy(
                            out=out.rearrange("p (h e i) t -> p h e t i", h=count, i=RUN),
                            in_=source.rearrange(
                                "p t (h c e i) -> p c h e t i", h=count, c=PARTS, i=RUN
                            )[:, part],
                        )
                column += heads * D

        def quantise(b, g, cols=slice(0, N_BLOCK)):
            if (b, g) not in w_codes:
                w_codes[(b, g)] = keep.tile(
                    [P, width(b)], U32, name="w_codes%d_%d" % (b, g), align_bytes=64
                )
                w_scales[(b, g)] = keep.tile(
                    [P, width(b)], U8, name="w_scales%d_%d" % (b, g), align_bytes=64
                )
            nc.vector.quantize_mx(
                out=w_codes[(b, g)][:, cols].bitcast(FP8X4),
                scales=w_scales[(b, g)][:, cols],
                in_=w_grouped[(b, g)][:, cols, :].rearrange("p n t -> p (n t)"),
            )

        def multiply(b, m, g, cols=slice(0, N_BLOCK)):
            if (b, m) not in acc:
                acc[(b, m)] = psum.tile([P, width(b)], F32, name="acc", tag="bank")
            nc.tensor.matmul_mx(
                out=acc[(b, m)][:, cols],
                lhsT=x_codes[m][:, g, :].bitcast(FP8X4),
                lhsT_scale=x_scales[m][:, g, :],
                rhs=w_codes[(b, g)][:, cols].bitcast(FP8X4),
                rhs_scale=w_scales[(b, g)][:, cols],
                start=(g == 0),
                stop=(g == PASSES - 1),
            )

        def empty(b, m, by="scalar"):
            res = keep.tile([P, width(b)], F32, name="res%d_%d" % (b, m))
            if by == "vector":
                nc.vector.tensor_copy(out=res[:], in_=acc[(b, m)][:])
            else:
                nc.scalar.copy(out=res[:], in_=acc[(b, m)][:])
            column = 0
            for head, heads, part in BLOCKS[b]:
                nc.sync.dma_start(
                    out=out_rows[part][m * P : (m + 1) * P, head * D : (head + heads) * D],
                    in_=res[:, column : column + heads * D],
                )
                column += heads * D

        def multiply_all(b, g, cols=slice(0, N_BLOCK)):
            for m in range(ROW_TILES):
                multiply(b, m, g, cols)

        def empty_all(b, shared=False):
            for m in range(ROW_TILES):
                empty(b, m, by="vector" if shared and m % 2 == 0 else "scalar")

        warm = psum.tile([P, N_BLOCK], F32, name="warm", tag="bank")

        def keep_warm(times):
            for i in range(times):
                nc.tensor.matmul(
                    out=warm[:], lhsT=ones[:], rhs=gain_row[:, :N_BLOCK], start=True, stop=True
                )

        square(0)
        square_vector(1)
        root(0, 1)
        spread_gain()
        square(2)
        normalise(0)
        transpose_x(0)
        root(1, 2)
        square(3)
        normalise(1)
        transpose_x(1)
        root(2, 3)
        normalise(2)
        root(3, 4)
        normalise(3)
        transpose_x(2)
        transpose_x(3)
        regroup_x(0)
        regroup_x(1)
        regroup(1, 0, by="scalar", head_range=(0, 2))
        regroup_x(2)
        regroup_x(3)
        regroup(0, 0)
        quantise_x(0)
        quantise_x(1)
        quantise(0, 0)
        quantise_x(2)
        quantise_x(3)
        keep_warm(4)
        multiply_all(0, 0)
        keep_warm(3)
        regroup(1, 0, by="scalar", head_range=(2, 4))
        regroup(0, 1)
        quantise(1, 0)
        quantise(0, 1)
        multiply_all(0, 1)
        regroup(1, 1, by="scalar")
        regroup(2, 0, by="scalar", head_range=(0, 2))
        empty_all(0)
        multiply_all(1, 0)
        quantise(1, 1)
        multiply_all(1, 1)
        regroup(2, 0, head_range=(2, 4))
        regroup(2, 1)
        empty_all(1)
        regroup(4, 0, by="scalar", head_range=(4, 6))
        quantise(2, 0)
        multiply_all(2, 0)
        regroup(3, 0)
        quantise(2, 1)
        multiply_all(2, 1)
        empty_all(2)
        regroup(5, 0, by="scalar", head_range=(4, 6))
        regroup(3, 1)
        quantise(3, 0)
        multiply_all(3, 0)
        regroup(4, 0, head_range=(6, 8))
        quantise(3, 1)
        multiply_all(3, 1)
        empty_all(3)
        regroup(4, 1)
        quantise(4, 0)
        multiply_all(4, 0)
        regroup(5, 0, head_range=(6, 8))
        quantise(4, 1)
        multiply_all(4, 1)
        empty_all(4)
        quantise(5, 0)
        multiply_all(5, 0)
        regroup(5, 1)
        quantise(5, 1)
        multiply_all(5, 1)
        empty_all(5, shared=True)
